import numpy as np
import ml_dtypes


def mxq(x, axis, fmt="e4m3"):
    dtype, down = {"e4m3": (ml_dtypes.float8_e4m3fn, 7), "e5m2": (ml_dtypes.float8_e5m2, 14)}[fmt]
    v = np.moveaxis(np.asarray(x, np.float32).astype(ml_dtypes.bfloat16).astype(np.float64), axis, -1)
    blocks = v.reshape(v.shape[:-1] + (-1, 32))
    amax = np.abs(blocks).max(-1, keepdims=True)
    byte = np.maximum(np.where(amax > 0, np.frexp(amax)[1] - 1 + 127, 0) - down, 1)
    scale = np.exp2(byte - 127.0)
    codes = (blocks / scale).astype(np.float32).astype(dtype).astype(np.float64)
    return np.moveaxis((codes * scale).reshape(v.shape), -1, axis)


WIDE = False


def mx_kscale(k):
    if not WIDE:
        return np.ones(k)
    levels = np.array([10, -10, 5, -5, 0])
    a = np.random.permutation(np.resize(levels, k // 512 * 4)).reshape(k // 512, 4)
    idx = np.arange(k)
    return np.exp2(a[idx // 512, idx % 128 // 32])


BF16 = ml_dtypes.bfloat16


def bf(x):
    return np.asarray(x, np.float32).astype(BF16)


def f64(x):
    return np.asarray(x).astype(np.float64)


B, V, QK, DK, HC, WC, HS, WS = 4, 512, 512, 256, 64, 64, 32, 16
LQ = HC * WC
EPS = 1e-5
QS = np.sqrt(2.0) / DK ** 0.25


def mvn(x):
    mean = x.mean(axis=2, keepdims=True)
    var = x.var(axis=2, ddof=1, keepdims=True) + EPS
    return (x - mean) / np.sqrt(var)


def setup_inputs():
    s = mx_kscale(QK)
    g = 2.0 ** np.random.uniform(-9.0, 1.0, QK) * np.minimum(s, 1.0) ** 3
    f = g / np.sqrt(g * g + EPS)
    mu = 0.5 * np.random.standard_normal(QK)
    return {"c_1x": bf((np.random.standard_normal((B, QK, HC, WC)) + mu[None, :, None, None]) * g[None, :, None, None]),
            "f_w": bf(np.random.standard_normal((DK, QK)) * QS / np.sqrt(QK) / f[None, :]),
            "f_b": bf(np.random.standard_normal(DK) * 0.1)}


def reference(c_1x, f_w, f_b):
    xn = mvn(f64(c_1x).reshape(B, QK, LQ))
    y = (mxq(f64(f_w), 1, "e4m3") @ mxq(xn, 1, "e4m3")) + f64(f_b)[None, :, None]
    return y.transpose(0, 2, 1)

@@ -1,0 +1,177 @@
+from contextlib import ExitStack
+
+import concourse.mybir as mybir
+from concourse.masks import make_identity
+
+BF16 = mybir.dt.bfloat16
+F32 = mybir.dt.float32
+U32 = mybir.dt.uint32
+U8 = mybir.dt.uint8
+FP8X4 = mybir.dt.float8_e4m3fn_x4
+ALU = mybir.AluOpType
+ACT = mybir.ActivationFunctionType
+
+P = 128
+PACK = 4
+BATCH = 4
+PIXELS = 64 * 64
+OUT_CH = 256
+EPS = 1e-5
+
+STAT_SLICE = 512
+STAT_SLICES = PIXELS // STAT_SLICE
+VECTOR_ROWS = 3
+CHUNK = 512
+CHUNKS = PIXELS // CHUNK
+RUN = 4
+PIXEL_TILE = P
+BANK_TILES = 2
+
+FLOPS = 2 * BATCH * PIXELS * P * PACK * OUT_CH
+
+
+def load_batch(nc, x_tile, c_1x, b):
+    rows = c_1x[b, :, :, :].rearrange("(p t) h w -> t p (h w)", t=PACK)
+    for t in range(PACK):
+        nc.sync.dma_start(out=x_tile[:, t, :], in_=rows[t, :, :])
+
+
+def quantise_weights(nc, const, psum_w, f_w):
+    halves = OUT_CH // P
+    w_rows = const.tile([P, halves, P * PACK], BF16)
+    nc.scalar.dma_start(out=w_rows[:], in_=f_w.rearrange("(h o) c -> o h c", h=halves))
+    identity = const.tile([P, P], BF16)
+    make_identity(nc, identity[:])
+    w_sorted = const.tile([P, halves, PACK, P], BF16)
+    nc.scalar.copy(out=w_sorted[:], in_=w_rows[:].rearrange("o h (q t) -> o h t q", t=PACK))
+    w_turned = psum_w.tile([P, PACK, OUT_CH], BF16)
+    for h in range(halves):
+        for t in range(PACK):
+            nc.tensor.transpose(w_turned[:, t, h * P : (h + 1) * P], w_sorted[:, h, t, :], identity[:])
+    w_grouped = const.tile([P, OUT_CH, PACK], BF16, align_bytes=64)
+    nc.scalar.copy(out=w_grouped[:], in_=w_turned[:].rearrange("q t o -> q o t"))
+    w_codes = const.tile([P, OUT_CH], U32, align_bytes=64)
+    w_scales = const.tile([P, OUT_CH], U8, align_bytes=64)
+    nc.vector.quantize_mx(
+        out=w_codes[:].bitcast(FP8X4),
+        scales=w_scales[:],
+        in_=w_grouped[:].rearrange("q o t -> q (o t)"),
+    )
+    return w_codes, w_scales
+
+
+def load_bias(nc, const, f_b):
+    bias_bf16 = const.tile([P, OUT_CH], BF16)
+    nc.sync.dma_start(out=bias_bf16[:], in_=f_b.partition_broadcast(P))
+    bias = const.tile([P, BANK_TILES, OUT_CH], F32)
+    for g in range(BANK_TILES):
+        nc.vector.tensor_copy(out=bias[:, g, :], in_=bias_bf16[:])
+    return bias
+
+
+def statistics(nc, small, scratch, x_tile):
+    stats = small.tile([P, VECTOR_ROWS, STAT_SLICES, 6], F32)
+    mean_var = small.tile([P, VECTOR_ROWS, 2], F32)
+    for t in range(VECTOR_ROWS):
+        for s in range(STAT_SLICES):
+            nc.vector.bn_stats(
+                out=stats[:, t, s, :], in_=x_tile[:, t, s * STAT_SLICE : (s + 1) * STAT_SLICE]
+            )
+        nc.vector.bn_aggr(out=mean_var[:, t, :], in_=stats[:, t, :, :].rearrange("p s k -> p (s k)"))
+    x_row = x_tile[:, VECTOR_ROWS, :]
+    total = small.tile([P, 1], F32)
+    unread_a = scratch.tile([P, PIXELS], BF16, tag="unread")
+    nc.scalar.activation(out=unread_a[:], in_=x_row, func=ACT.Identity, accum_out=total[:])
+    mean_row3 = small.tile([P, 1], F32)
+    nc.scalar.mul(out=mean_row3[:], in_=total[:], mul=1.0 / PIXELS)
+    squares = small.tile([P, 1], F32)
+    unread_b = scratch.tile([P, PIXELS], BF16, tag="unread")
+    nc.scalar.activation(
+        out=unread_b[:], in_=x_row, func=ACT.Square, scale=-1.0, bias=mean_row3[:], accum_out=squares[:]
+    )
+    std = small.tile([P, PACK], F32)
+    nc.scalar.activation(
+        out=std[:, 0:VECTOR_ROWS],
+        in_=mean_var[:, :, 1],
+        func=ACT.Sqrt,
+        scale=PIXELS / (PIXELS - 1.0),
+        bias=EPS,
+    )
+    nc.scalar.activation(
+        out=std[:, VECTOR_ROWS:PACK], in_=squares[:], func=ACT.Sqrt, scale=1.0 / (PIXELS - 1.0), bias=EPS
+    )
+    rstd = small.tile([P, PACK], F32)
+    nc.vector.reciprocal(out=rstd[:], in_=std[:])
+    means = [mean_var[:, t, 0:1] for t in range(VECTOR_ROWS)] + [mean_row3[:]]
+    return means, rstd
+
+
+def tile_adaattn_pa_t_kernel(tc, c_1x, f_w, f_b, out):
+    nc = tc.nc
+    with ExitStack() as ctx:
+        const = ctx.enter_context(tc.tile_pool(name="const", bufs=1))
+        x_pool = ctx.enter_context(tc.tile_pool(name="x", bufs=BATCH))
+        small = ctx.enter_context(tc.tile_pool(name="small", bufs=BATCH))
+        scratch = ctx.enter_context(tc.tile_pool(name="scratch", bufs=2))
+        stage = ctx.enter_context(tc.tile_pool(name="stage", bufs=4))
+        psum_w = ctx.enter_context(tc.psum_pool(name="psum_w", bufs=1))
+        psum = ctx.enter_context(tc.psum_pool(name="psum", bufs=6))
+
+        w_codes, w_scales = quantise_weights(nc, const, psum_w, f_w)
+        x_tiles = []
+        for b in range(BATCH):
+            x_tile = x_pool.tile([P, PACK, PIXELS], BF16)
+            load_batch(nc, x_tile, c_1x, b)
+            x_tiles.append(x_tile)
+            if b == 1:
+                bias = load_bias(nc, const, f_b)
+
+        for b in range(BATCH):
+            x_tile = x_tiles[b]
+            means, rstd = statistics(nc, small, scratch, x_tile)
+            for t in range(PACK):
+                nc.vector.tensor_scalar(
+                    out=x_tile[:, t, :],
+                    in0=x_tile[:, t, :],
+                    scalar1=means[t],
+                    scalar2=rstd[:, t : t + 1],
+                    op0=ALU.subtract,
+                    op1=ALU.mult,
+                )
+            for j in range(CHUNKS):
+                pixels = slice(j * CHUNK, (j + 1) * CHUNK)
+                grouped = stage.tile([P, CHUNK, PACK], BF16, align_bytes=64)
+                nc.scalar.copy(
+                    out=grouped[:].rearrange("p (c i) t -> p c t i", i=RUN),
+                    in_=x_tile[:, :, pixels].rearrange("p t (c i) -> p c t i", i=RUN),
+                )
+                codes = stage.tile([P, CHUNK], U32, align_bytes=64)
+                scales = stage.tile([P, CHUNK], U8, align_bytes=64)
+                nc.vector.quantize_mx(
+                    out=codes[:].bitcast(FP8X4),
+                    scales=scales[:],
+                    in_=grouped[:].rearrange("p w t -> p (w t)"),
+                )
+                result = stage.tile([P, CHUNK // PIXEL_TILE, OUT_CH], F32)
+                for h in range(CHUNK // (PIXEL_TILE * BANK_TILES)):
+                    acc = psum.tile([P, BANK_TILES, OUT_CH], F32)
+                    for g in range(BANK_TILES):
+                        first = (h * BANK_TILES + g) * PIXEL_TILE
+                        nc.tensor.matmul_mx(
+                            out=acc[:, g, :],
+                            lhsT=codes[:, first : first + PIXEL_TILE].bitcast(FP8X4),
+                            lhsT_scale=scales[:, first : first + PIXEL_TILE],
+                            rhs=w_codes[:].bitcast(FP8X4),
+                            rhs_scale=w_scales[:],
+                            start=True,
+                            stop=True,
+                        )
+                    nc.vector.tensor_tensor(
+                        out=result[:, h * BANK_TILES : (h + 1) * BANK_TILES, :],
+                        in0=acc[:],
+                        in1=bias[:],
+                        op=ALU.add,
+                    )
+                nc.sync.dma_start(
+                    out=out[b, pixels, :].rearrange("(g p) o -> p g o", p=PIXEL_TILE), in_=result[:]
+                )

@@ -113,6 +113,7 @@ def tile_adaattn_pa_t_kernel(tc, c_1x, f_w, f_b, out):
         x_pool = ctx.enter_context(tc.tile_pool(name="x", bufs=BATCH))
         small = ctx.enter_context(tc.tile_pool(name="small", bufs=BATCH))
         scratch = ctx.enter_context(tc.tile_pool(name="scratch", bufs=2))
+        group_pool = ctx.enter_context(tc.tile_pool(name="grouped", bufs=8))
         stage = ctx.enter_context(tc.tile_pool(name="stage", bufs=4))
         psum_w = ctx.enter_context(tc.psum_pool(name="psum_w", bufs=1))
         psum = ctx.enter_context(tc.psum_pool(name="psum", bufs=6))
@@ -126,7 +127,7 @@ def tile_adaattn_pa_t_kernel(tc, c_1x, f_w, f_b, out):
             if b == 1:
                 bias = load_bias(nc, const, f_b)
 
-        for b in range(BATCH):
+        def prepare(b):
             x_tile = x_tiles[b]
             means, rstd = statistics(nc, small, scratch, x_tile)
             for t in range(PACK):
@@ -138,40 +139,48 @@ def tile_adaattn_pa_t_kernel(tc, c_1x, f_w, f_b, out):
                     op0=ALU.subtract,
                     op1=ALU.mult,
                 )
-            for j in range(CHUNKS):
-                pixels = slice(j * CHUNK, (j + 1) * CHUNK)
-                grouped = stage.tile([P, CHUNK, PACK], BF16, align_bytes=64)
-                nc.scalar.copy(
-                    out=grouped[:].rearrange("p (c i) t -> p c t i", i=RUN),
-                    in_=x_tile[:, :, pixels].rearrange("p t (c i) -> p c t i", i=RUN),
-                )
-                codes = stage.tile([P, CHUNK], U32, align_bytes=64)
-                scales = stage.tile([P, CHUNK], U8, align_bytes=64)
-                nc.vector.quantize_mx(
-                    out=codes[:].bitcast(FP8X4),
-                    scales=scales[:],
-                    in_=grouped[:].rearrange("p w t -> p (w t)"),
-                )
-                result = stage.tile([P, CHUNK // PIXEL_TILE, OUT_CH], F32)
-                for h in range(CHUNK // (PIXEL_TILE * BANK_TILES)):
-                    acc = psum.tile([P, BANK_TILES, OUT_CH], F32)
-                    for g in range(BANK_TILES):
-                        first = (h * BANK_TILES + g) * PIXEL_TILE
-                        nc.tensor.matmul_mx(
-                            out=acc[:, g, :],
-                            lhsT=codes[:, first : first + PIXEL_TILE].bitcast(FP8X4),
-                            lhsT_scale=scales[:, first : first + PIXEL_TILE],
-                            rhs=w_codes[:].bitcast(FP8X4),
-                            rhs_scale=w_scales[:],
-                            start=True,
-                            stop=True,
-                        )
-                    nc.vector.tensor_tensor(
-                        out=result[:, h * BANK_TILES : (h + 1) * BANK_TILES, :],
-                        in0=acc[:],
-                        in1=bias[:],
-                        op=ALU.add,
+
+        def convolve(b, j):
+            pixels = slice(j * CHUNK, (j + 1) * CHUNK)
+            grouped = group_pool.tile([P, CHUNK, PACK], BF16, align_bytes=64)
+            nc.scalar.copy(
+                out=grouped[:].rearrange("p (c i) t -> p c t i", i=RUN),
+                in_=x_tiles[b][:, :, pixels].rearrange("p t (c i) -> p c t i", i=RUN),
+            )
+            codes = stage.tile([P, CHUNK], U32, align_bytes=64)
+            scales = stage.tile([P, CHUNK], U8, align_bytes=64)
+            nc.vector.quantize_mx(
+                out=codes[:].bitcast(FP8X4),
+                scales=scales[:],
+                in_=grouped[:].rearrange("p w t -> p (w t)"),
+            )
+            result = stage.tile([P, CHUNK // PIXEL_TILE, OUT_CH], F32)
+            for h in range(CHUNK // (PIXEL_TILE * BANK_TILES)):
+                acc = psum.tile([P, BANK_TILES, OUT_CH], F32)
+                for g in range(BANK_TILES):
+                    first = (h * BANK_TILES + g) * PIXEL_TILE
+                    nc.tensor.matmul_mx(
+                        out=acc[:, g, :],
+                        lhsT=codes[:, first : first + PIXEL_TILE].bitcast(FP8X4),
+                        lhsT_scale=scales[:, first : first + PIXEL_TILE],
+                        rhs=w_codes[:].bitcast(FP8X4),
+                        rhs_scale=w_scales[:],
+                        start=True,
+                        stop=True,
                     )
-                nc.sync.dma_start(
-                    out=out[b, pixels, :].rearrange("(g p) o -> p g o", p=PIXEL_TILE), in_=result[:]
+                nc.vector.tensor_tensor(
+                    out=result[:, h * BANK_TILES : (h + 1) * BANK_TILES, :],
+                    in0=acc[:],
+                    in1=bias[:],
+                    op=ALU.add,
                 )
+            nc.sync.dma_start(
+                out=out[b, pixels, :].rearrange("(g p) o -> p g o", p=PIXEL_TILE), in_=result[:]
+            )
+
+        prepare(0)
+        for b in range(BATCH):
+            if b + 1 < BATCH:
+                prepare(b + 1)
+            for j in range(CHUNKS):
+                convolve(b, j)

@@ -18,22 +18,27 @@ PIXELS = 64 * 64
 OUT_CH = 256
 EPS = 1e-5
 
+LOAD_PIECES = 2
 STAT_SLICE = 512
 STAT_SLICES = PIXELS // STAT_SLICE
-VECTOR_ROWS = 3
+SCALAR_EVERY = 3
 CHUNK = 512
 CHUNKS = PIXELS // CHUNK
 RUN = 4
 PIXEL_TILE = P
 BANK_TILES = 2
+BANK_PIXELS = BANK_TILES * PIXEL_TILE
 
 FLOPS = 2 * BATCH * PIXELS * P * PACK * OUT_CH
 
 
 def load_batch(nc, x_tile, c_1x, b):
     rows = c_1x[b, :, :, :].rearrange("(p t) h w -> t p (h w)", t=PACK)
+    piece = PIXELS // LOAD_PIECES
     for t in range(PACK):
-        nc.sync.dma_start(out=x_tile[:, t, :], in_=rows[t, :, :])
+        for i in range(LOAD_PIECES):
+            pixels = slice(i * piece, (i + 1) * piece)
+            nc.sync.dma_start(out=x_tile[:, t, pixels], in_=rows[t, :, pixels])
 
 
 def quantise_weights(nc, const, psum_w, f_w):
@@ -69,41 +74,27 @@ def load_bias(nc, const, f_b):
     return bias
 
 
-def statistics(nc, small, scratch, x_tile):
-    stats = small.tile([P, VECTOR_ROWS, STAT_SLICES, 6], F32)
-    mean_var = small.tile([P, VECTOR_ROWS, 2], F32)
-    for t in range(VECTOR_ROWS):
-        for s in range(STAT_SLICES):
-            nc.vector.bn_stats(
-                out=stats[:, t, s, :], in_=x_tile[:, t, s * STAT_SLICE : (s + 1) * STAT_SLICE]
-            )
-        nc.vector.bn_aggr(out=mean_var[:, t, :], in_=stats[:, t, :, :].rearrange("p s k -> p (s k)"))
-    x_row = x_tile[:, VECTOR_ROWS, :]
+def row_statistics_on_vector(nc, small, x_row):
+    stats = small.tile([P, STAT_SLICES, 6], F32)
+    for s in range(STAT_SLICES):
+        nc.vector.bn_stats(out=stats[:, s, :], in_=x_row[:, s * STAT_SLICE : (s + 1) * STAT_SLICE])
+    mean_var = small.tile([P, 2], F32)
+    nc.vector.bn_aggr(out=mean_var[:], in_=stats[:].rearrange("p s k -> p (s k)"))
+    return mean_var[:, 0:1], mean_var[:, 1:2], PIXELS / (PIXELS - 1.0)
+
+
+def row_statistics_on_scalar(nc, small, scratch, x_row):
     total = small.tile([P, 1], F32)
     unread_a = scratch.tile([P, PIXELS], BF16, tag="unread")
     nc.scalar.activation(out=unread_a[:], in_=x_row, func=ACT.Identity, accum_out=total[:])
-    mean_row3 = small.tile([P, 1], F32)
-    nc.scalar.mul(out=mean_row3[:], in_=total[:], mul=1.0 / PIXELS)
+    mean = small.tile([P, 1], F32)
+    nc.scalar.mul(out=mean[:], in_=total[:], mul=1.0 / PIXELS)
     squares = small.tile([P, 1], F32)
     unread_b = scratch.tile([P, PIXELS], BF16, tag="unread")
     nc.scalar.activation(
-        out=unread_b[:], in_=x_row, func=ACT.Square, scale=-1.0, bias=mean_row3[:], accum_out=squares[:]
+        out=unread_b[:], in_=x_row, func=ACT.Square, scale=-1.0, bias=mean[:], accum_out=squares[:]
     )
-    std = small.tile([P, PACK], F32)
-    nc.scalar.activation(
-        out=std[:, 0:VECTOR_ROWS],
-        in_=mean_var[:, :, 1],
-        func=ACT.Sqrt,
-        scale=PIXELS / (PIXELS - 1.0),
-        bias=EPS,
-    )
-    nc.scalar.activation(
-        out=std[:, VECTOR_ROWS:PACK], in_=squares[:], func=ACT.Sqrt, scale=1.0 / (PIXELS - 1.0), bias=EPS
-    )
-    rstd = small.tile([P, PACK], F32)
-    nc.vector.reciprocal(out=rstd[:], in_=std[:])
-    means = [mean_var[:, t, 0:1] for t in range(VECTOR_ROWS)] + [mean_row3[:]]
-    return means, rstd
+    return mean[:], squares[:], 1.0 / (PIXELS - 1.0)
 
 
 def tile_adaattn_pa_t_kernel(tc, c_1x, f_w, f_b, out):
@@ -111,7 +102,7 @@ def tile_adaattn_pa_t_kernel(tc, c_1x, f_w, f_b, out):
     with ExitStack() as ctx:
         const = ctx.enter_context(tc.tile_pool(name="const", bufs=1))
         x_pool = ctx.enter_context(tc.tile_pool(name="x", bufs=BATCH))
-        small = ctx.enter_context(tc.tile_pool(name="small", bufs=BATCH))
+        small = ctx.enter_context(tc.tile_pool(name="small", bufs=2 * PACK))
         scratch = ctx.enter_context(tc.tile_pool(name="scratch", bufs=2))
         group_pool = ctx.enter_context(tc.tile_pool(name="grouped", bufs=8))
         stage = ctx.enter_context(tc.tile_pool(name="stage", bufs=4))
@@ -129,7 +120,18 @@ def tile_adaattn_pa_t_kernel(tc, c_1x, f_w, f_b, out):
 
         def prepare(b):
             x_tile = x_tiles[b]
-            means, rstd = statistics(nc, small, scratch, x_tile)
+            std = small.tile([P, PACK], F32)
+            means = []
+            for t in range(PACK):
+                x_row = x_tile[:, t, :]
+                if (b * PACK + t) % SCALAR_EVERY == SCALAR_EVERY - 1:
+                    mean, spread, factor = row_statistics_on_scalar(nc, small, scratch, x_row)
+                else:
+                    mean, spread, factor = row_statistics_on_vector(nc, small, x_row)
+                means.append(mean)
+                nc.scalar.activation(out=std[:, t : t + 1], in_=spread, func=ACT.Sqrt, scale=factor, bias=EPS)
+            rstd = small.tile([P, PACK], F32)
+            nc.vector.reciprocal(out=rstd[:], in_=std[:])
             for t in range(PACK):
                 nc.vector.tensor_scalar(
                     out=x_tile[:, t, :],
@@ -141,11 +143,11 @@ def tile_adaattn_pa_t_kernel(tc, c_1x, f_w, f_b, out):
                 )
 
         def convolve(b, j):
-            pixels = slice(j * CHUNK, (j + 1) * CHUNK)
+            first_pixel = j * CHUNK
             grouped = group_pool.tile([P, CHUNK, PACK], BF16, align_bytes=64)
             nc.scalar.copy(
                 out=grouped[:].rearrange("p (c i) t -> p c t i", i=RUN),
-                in_=x_tiles[b][:, :, pixels].rearrange("p t (c i) -> p c t i", i=RUN),
+                in_=x_tiles[b][:, :, first_pixel : first_pixel + CHUNK].rearrange("p t (c i) -> p c t i", i=RUN),
             )
             codes = stage.tile([P, CHUNK], U32, align_bytes=64)
             scales = stage.tile([P, CHUNK], U8, align_bytes=64)
@@ -154,11 +156,10 @@ def tile_adaattn_pa_t_kernel(tc, c_1x, f_w, f_b, out):
                 scales=scales[:],
                 in_=grouped[:].rearrange("p w t -> p (w t)"),
             )
-            result = stage.tile([P, CHUNK // PIXEL_TILE, OUT_CH], F32)
-            for h in range(CHUNK // (PIXEL_TILE * BANK_TILES)):
+            for h in range(CHUNK // BANK_PIXELS):
                 acc = psum.tile([P, BANK_TILES, OUT_CH], F32)
                 for g in range(BANK_TILES):
-                    first = (h * BANK_TILES + g) * PIXEL_TILE
+                    first = h * BANK_PIXELS + g * PIXEL_TILE
                     nc.tensor.matmul_mx(
                         out=acc[:, g, :],
                         lhsT=codes[:, first : first + PIXEL_TILE].bitcast(FP8X4),
@@ -168,15 +169,13 @@ def tile_adaattn_pa_t_kernel(tc, c_1x, f_w, f_b, out):
                         start=True,
                         stop=True,
                     )
-                nc.vector.tensor_tensor(
-                    out=result[:, h * BANK_TILES : (h + 1) * BANK_TILES, :],
-                    in0=acc[:],
-                    in1=bias[:],
-                    op=ALU.add,
+                result = stage.tile([P, BANK_TILES, OUT_CH], F32)
+                nc.vector.tensor_tensor(out=result[:], in0=acc[:], in1=bias[:], op=ALU.add)
+                stored = first_pixel + h * BANK_PIXELS
+                nc.sync.dma_start(
+                    out=out[b, stored : stored + BANK_PIXELS, :].rearrange("(g p) o -> p g o", p=PIXEL_TILE),
+                    in_=result[:],
                 )
-            nc.sync.dma_start(
-                out=out[b, pixels, :].rearrange("(g p) o -> p g o", p=PIXEL_TILE), in_=result[:]
-            )
 
         prepare(0)
         for b in range(BATCH):

@@ -21,7 +21,7 @@ EPS = 1e-5
 LOAD_PIECES = 2
 STAT_SLICE = 512
 STAT_SLICES = PIXELS // STAT_SLICE
-SCALAR_EVERY = 3
+POOL_PIXELS = 192
 CHUNK = 512
 CHUNKS = PIXELS // CHUNK
 RUN = 4
@@ -30,6 +30,10 @@ BANK_TILES = 2
 BANK_PIXELS = BANK_TILES * PIXEL_TILE
 
 FLOPS = 2 * BATCH * PIXELS * P * PACK * OUT_CH
+
+
+def scalar_takes_row(row):
+    return row == 2 or (row > PACK and row % 2 == 1)
 
 
 def load_batch(nc, x_tile, c_1x, b):
@@ -124,7 +128,7 @@ def tile_adaattn_pa_t_kernel(tc, c_1x, f_w, f_b, out):
             means = []
             for t in range(PACK):
                 x_row = x_tile[:, t, :]
-                if (b * PACK + t) % SCALAR_EVERY == SCALAR_EVERY - 1:
+                if scalar_takes_row(b * PACK + t):
                     mean, spread, factor = row_statistics_on_scalar(nc, small, scratch, x_row)
                 else:
                     mean, spread, factor = row_statistics_on_vector(nc, small, x_row)
@@ -145,9 +149,18 @@ def tile_adaattn_pa_t_kernel(tc, c_1x, f_w, f_b, out):
         def convolve(b, j):
             first_pixel = j * CHUNK
             grouped = group_pool.tile([P, CHUNK, PACK], BF16, align_bytes=64)
+            split = CHUNK - POOL_PIXELS
             nc.scalar.copy(
-                out=grouped[:].rearrange("p (c i) t -> p c t i", i=RUN),
-                in_=x_tiles[b][:, :, first_pixel : first_pixel + CHUNK].rearrange("p t (c i) -> p c t i", i=RUN),
+                out=grouped[:, :split, :].rearrange("p (c i) t -> p c t i", i=RUN),
+                in_=x_tiles[b][:, :, first_pixel : first_pixel + split].rearrange("p t (c i) -> p c t i", i=RUN),
+            )
+            nc.gpsimd.tensor_scalar(
+                out=grouped[:, split:, :],
+                in0=x_tiles[b][:, :, first_pixel + split : first_pixel + CHUNK].rearrange("p t w -> p w t"),
+                scalar1=1.0,
+                scalar2=0.0,
+                op0=ALU.mult,
+                op1=ALU.add,
             )
             codes = stage.tile([P, CHUNK], U32, align_bytes=64)
             scales = stage.tile([P, CHUNK], U8, align_bytes=64)

@@ -14,6 +14,7 @@ ACT = mybir.ActivationFunctionType
 P = 128
 PACK = 4
 BATCH = 4
+ROWS = BATCH * PACK
 PIXELS = 64 * 64
 OUT_CH = 256
 EPS = 1e-5
@@ -21,19 +22,34 @@ EPS = 1e-5
 LOAD_PIECES = 2
 STAT_SLICE = 512
 STAT_SLICES = PIXELS // STAT_SLICE
-POOL_PIXELS = 192
 CHUNK = 512
 CHUNKS = PIXELS // CHUNK
+ALL_CHUNKS = BATCH * CHUNKS
+NORM_PIECES = 2
+NORM_PIXELS = PIXELS // NORM_PIECES
 RUN = 4
 PIXEL_TILE = P
 BANK_TILES = 2
 BANK_PIXELS = BANK_TILES * PIXEL_TILE
+RING = 3
+POOL_LONG = 448
+POOL_SHORT = 256
+POOL_LAST = 128
+NORM_STEP = 12
+FOLD = 512
+LEAD = NORM_STEP + 1 + RING
 
 FLOPS = 2 * BATCH * PIXELS * P * PACK * OUT_CH
 
 
-def scalar_takes_row(row):
-    return row == 2 or (row > PACK and row % 2 == 1)
+def kind_of(row):
+    if row < PACK:
+        return "scalar" if row == 1 else "vector"
+    return "tensor" if row % PACK == 0 else "shared"
+
+
+def vector_alone(row):
+    return kind_of(row) == "vector"
 
 
 def load_batch(nc, x_tile, c_1x, b):
@@ -45,7 +61,7 @@ def load_batch(nc, x_tile, c_1x, b):
             nc.sync.dma_start(out=x_tile[:, t, pixels], in_=rows[t, :, pixels])
 
 
-def quantise_weights(nc, const, psum_w, f_w):
+def turn_weights(nc, const, psum_w, f_w):
     halves = OUT_CH // P
     w_rows = const.tile([P, halves, P * PACK], BF16)
     nc.scalar.dma_start(out=w_rows[:], in_=f_w.rearrange("(h o) c -> o h c", h=halves))
@@ -59,46 +75,7 @@ def quantise_weights(nc, const, psum_w, f_w):
             nc.tensor.transpose(w_turned[:, t, h * P : (h + 1) * P], w_sorted[:, h, t, :], identity[:])
     w_grouped = const.tile([P, OUT_CH, PACK], BF16, align_bytes=64)
     nc.scalar.copy(out=w_grouped[:], in_=w_turned[:].rearrange("q t o -> q o t"))
-    w_codes = const.tile([P, OUT_CH], U32, align_bytes=64)
-    w_scales = const.tile([P, OUT_CH], U8, align_bytes=64)
-    nc.vector.quantize_mx(
-        out=w_codes[:].bitcast(FP8X4),
-        scales=w_scales[:],
-        in_=w_grouped[:].rearrange("q o t -> q (o t)"),
-    )
-    return w_codes, w_scales
-
-
-def load_bias(nc, const, f_b):
-    bias_bf16 = const.tile([P, OUT_CH], BF16)
-    nc.sync.dma_start(out=bias_bf16[:], in_=f_b.partition_broadcast(P))
-    bias = const.tile([P, BANK_TILES, OUT_CH], F32)
-    for g in range(BANK_TILES):
-        nc.vector.tensor_copy(out=bias[:, g, :], in_=bias_bf16[:])
-    return bias
-
-
-def row_statistics_on_vector(nc, small, x_row):
-    stats = small.tile([P, STAT_SLICES, 6], F32)
-    for s in range(STAT_SLICES):
-        nc.vector.bn_stats(out=stats[:, s, :], in_=x_row[:, s * STAT_SLICE : (s + 1) * STAT_SLICE])
-    mean_var = small.tile([P, 2], F32)
-    nc.vector.bn_aggr(out=mean_var[:], in_=stats[:].rearrange("p s k -> p (s k)"))
-    return mean_var[:, 0:1], mean_var[:, 1:2], PIXELS / (PIXELS - 1.0)
-
-
-def row_statistics_on_scalar(nc, small, scratch, x_row):
-    total = small.tile([P, 1], F32)
-    unread_a = scratch.tile([P, PIXELS], BF16, tag="unread")
-    nc.scalar.activation(out=unread_a[:], in_=x_row, func=ACT.Identity, accum_out=total[:])
-    mean = small.tile([P, 1], F32)
-    nc.scalar.mul(out=mean[:], in_=total[:], mul=1.0 / PIXELS)
-    squares = small.tile([P, 1], F32)
-    unread_b = scratch.tile([P, PIXELS], BF16, tag="unread")
-    nc.scalar.activation(
-        out=unread_b[:], in_=x_row, func=ACT.Square, scale=-1.0, bias=mean[:], accum_out=squares[:]
-    )
-    return mean[:], squares[:], 1.0 / (PIXELS - 1.0)
+    return w_grouped, identity
 
 
 def tile_adaattn_pa_t_kernel(tc, c_1x, f_w, f_b, out):
@@ -106,50 +83,127 @@ def tile_adaattn_pa_t_kernel(tc, c_1x, f_w, f_b, out):
     with ExitStack() as ctx:
         const = ctx.enter_context(tc.tile_pool(name="const", bufs=1))
         x_pool = ctx.enter_context(tc.tile_pool(name="x", bufs=BATCH))
-        small = ctx.enter_context(tc.tile_pool(name="small", bufs=2 * PACK))
+        small = ctx.enter_context(tc.tile_pool(name="small", bufs=2))
         scratch = ctx.enter_context(tc.tile_pool(name="scratch", bufs=2))
-        group_pool = ctx.enter_context(tc.tile_pool(name="grouped", bufs=8))
-        stage = ctx.enter_context(tc.tile_pool(name="stage", bufs=4))
+        group_pool = ctx.enter_context(tc.tile_pool(name="grouped", bufs=RING))
+        stage = ctx.enter_context(tc.tile_pool(name="stage", bufs=3))
+        store_pool = ctx.enter_context(tc.tile_pool(name="stored", bufs=6))
         psum_w = ctx.enter_context(tc.psum_pool(name="psum_w", bufs=1))
+        psum_f = ctx.enter_context(tc.psum_pool(name="psum_f", bufs=1))
         psum = ctx.enter_context(tc.psum_pool(name="psum", bufs=6))
+        ctx.enter_context(tc.manual_schedule())
 
-        w_codes, w_scales = quantise_weights(nc, const, psum_w, f_w)
+        w_grouped, identity = turn_weights(nc, const, psum_w, f_w)
+        w_codes = const.tile([P, OUT_CH], U32, align_bytes=64)
+        w_scales = const.tile([P, OUT_CH], U8, align_bytes=64)
+        bias_bf16 = const.tile([P, OUT_CH], BF16)
+        bias = const.tile([P, BANK_TILES, OUT_CH], F32)
         x_tiles = []
         for b in range(BATCH):
             x_tile = x_pool.tile([P, PACK, PIXELS], BF16)
             load_batch(nc, x_tile, c_1x, b)
             x_tiles.append(x_tile)
             if b == 1:
-                bias = load_bias(nc, const, f_b)
+                nc.sync.dma_start(out=bias_bf16[:], in_=f_b.partition_broadcast(P))
 
-        def prepare(b):
-            x_tile = x_tiles[b]
-            std = small.tile([P, PACK], F32)
-            means = []
-            for t in range(PACK):
-                x_row = x_tile[:, t, :]
-                if scalar_takes_row(b * PACK + t):
-                    mean, spread, factor = row_statistics_on_scalar(nc, small, scratch, x_row)
-                else:
-                    mean, spread, factor = row_statistics_on_vector(nc, small, x_row)
-                means.append(mean)
-                nc.scalar.activation(out=std[:, t : t + 1], in_=spread, func=ACT.Sqrt, scale=factor, bias=EPS)
-            rstd = small.tile([P, PACK], F32)
-            nc.vector.reciprocal(out=rstd[:], in_=std[:])
-            for t in range(PACK):
+        mean = const.tile([P, ROWS], F32)
+        squares = const.tile([P, ROWS], F32)
+        mean_var = const.tile([P, ROWS, 2], F32)
+        std = const.tile([P, ROWS], F32)
+        rstd = const.tile([P, ROWS], F32)
+        grouped_of = {}
+        codes_of = {}
+        acc_of = {}
+
+        def x_row(row):
+            return x_tiles[row // PACK][:, row % PACK, :]
+
+        def mean_of(row):
+            if vector_alone(row):
+                return mean_var[:, row, 0:1]
+            return mean[:, row : row + 1]
+
+        def vector_statistics(row, half):
+            if vector_alone(row):
+                if half == 0:
+                    stats = small.tile([P, STAT_SLICES, 6], F32, name="stats")
+                    grouped_of["stats"] = stats
+                stats = grouped_of["stats"]
+                for s in range(half * STAT_SLICES // 2, (half + 1) * STAT_SLICES // 2):
+                    nc.vector.bn_stats(out=stats[:, s, :], in_=x_row(row)[:, s * STAT_SLICE : (s + 1) * STAT_SLICE])
+                if half == 1:
+                    nc.vector.bn_aggr(out=mean_var[:, row, :], in_=stats[:].rearrange("p s k -> p (s k)"))
+            elif half == 0 and kind_of(row) == "shared":
+                unread = scratch.tile([P, PIXELS], BF16, name="unread_v")
                 nc.vector.tensor_scalar(
-                    out=x_tile[:, t, :],
-                    in0=x_tile[:, t, :],
-                    scalar1=means[t],
-                    scalar2=rstd[:, t : t + 1],
+                    out=unread[:],
+                    in0=x_row(row),
+                    scalar1=1.0 / PIXELS,
+                    scalar2=None,
+                    op0=ALU.mult,
+                    op1=ALU.add,
+                    accum_out=mean[:, row : row + 1],
+                )
+
+        def tensor_fold(row):
+            folded = psum_f.tile([P, FOLD], F32, name="folded")
+            grouped_of["folded"] = folded
+            for s in range(PIXELS // FOLD):
+                nc.tensor.matmul(
+                    out=folded[:],
+                    lhsT=identity[:],
+                    rhs=x_row(row)[:, s * FOLD : (s + 1) * FOLD],
+                    start=(s == 0),
+                    stop=(s == PIXELS // FOLD - 1),
+                )
+
+        def scalar_mean(row):
+            source = grouped_of["folded"][:] if kind_of(row) == "tensor" else x_row(row)
+            unread = scratch.tile([P, PIXELS], BF16, name="unread_s")
+            nc.scalar.activation(
+                out=unread[:, : source.shape[1]],
+                in_=source,
+                func=ACT.Identity,
+                scale=1.0 / PIXELS,
+                accum_out=mean[:, row : row + 1],
+            )
+
+        def scalar_squares(row):
+            unread = scratch.tile([P, PIXELS], BF16, name="unread_s")
+            nc.scalar.activation(
+                out=unread[:],
+                in_=x_row(row),
+                func=ACT.Square,
+                scale=-1.0,
+                bias=mean[:, row : row + 1],
+                accum_out=squares[:, row : row + 1],
+            )
+
+        def scalar_std(row):
+            if vector_alone(row):
+                spread, factor = mean_var[:, row, 1:2], PIXELS / (PIXELS - 1.0)
+            else:
+                spread, factor = squares[:, row : row + 1], 1.0 / (PIXELS - 1.0)
+            nc.scalar.activation(out=std[:, row : row + 1], in_=spread, func=ACT.Sqrt, scale=factor, bias=EPS)
+
+        def normalise(b, piece):
+            pixels = slice(piece * NORM_PIXELS, (piece + 1) * NORM_PIXELS)
+            for t in range(PACK):
+                row = b * PACK + t
+                nc.vector.tensor_scalar(
+                    out=x_tiles[b][:, t, pixels],
+                    in0=x_tiles[b][:, t, pixels],
+                    scalar1=mean_of(row),
+                    scalar2=rstd[:, row : row + 1],
                     op0=ALU.subtract,
                     op1=ALU.mult,
                 )
 
-        def convolve(b, j):
-            first_pixel = j * CHUNK
-            grouped = group_pool.tile([P, CHUNK, PACK], BF16, align_bytes=64)
-            split = CHUNK - POOL_PIXELS
+        def regroup(chunk, pool_pixels):
+            b, first_pixel = chunk // CHUNKS, (chunk % CHUNKS) * CHUNK
+            grouped = group_pool.tile([P, CHUNK, PACK], BF16, align_bytes=64, name="grouped")
+            grouped_of[chunk] = grouped
+            split = CHUNK - pool_pixels
             nc.scalar.copy(
                 out=grouped[:, :split, :].rearrange("p (c i) t -> p c t i", i=RUN),
                 in_=x_tiles[b][:, :, first_pixel : first_pixel + split].rearrange("p t (c i) -> p c t i", i=RUN),
@@ -162,15 +216,19 @@ def tile_adaattn_pa_t_kernel(tc, c_1x, f_w, f_b, out):
                 op0=ALU.mult,
                 op1=ALU.add,
             )
-            codes = stage.tile([P, CHUNK], U32, align_bytes=64)
-            scales = stage.tile([P, CHUNK], U8, align_bytes=64)
+
+        def quantise_and_multiply(chunk):
+            codes = stage.tile([P, CHUNK], U32, align_bytes=64, name="codes")
+            scales = stage.tile([P, CHUNK], U8, align_bytes=64, name="scales")
             nc.vector.quantize_mx(
                 out=codes[:].bitcast(FP8X4),
                 scales=scales[:],
-                in_=grouped[:].rearrange("p w t -> p (w t)"),
+                in_=grouped_of[chunk][:].rearrange("p w t -> p (w t)"),
             )
+            acc_of[chunk] = []
             for h in range(CHUNK // BANK_PIXELS):
-                acc = psum.tile([P, BANK_TILES, OUT_CH], F32)
+                acc = psum.tile([P, BANK_TILES, OUT_CH], F32, name="acc")
+                acc_of[chunk].append(acc)
                 for g in range(BANK_TILES):
                     first = h * BANK_PIXELS + g * PIXEL_TILE
                     nc.tensor.matmul_mx(
@@ -182,17 +240,55 @@ def tile_adaattn_pa_t_kernel(tc, c_1x, f_w, f_b, out):
                         start=True,
                         stop=True,
                     )
-                result = stage.tile([P, BANK_TILES, OUT_CH], F32)
-                nc.vector.tensor_tensor(out=result[:], in0=acc[:], in1=bias[:], op=ALU.add)
+
+        def add_bias_and_store(chunk):
+            b, first_pixel = chunk // CHUNKS, (chunk % CHUNKS) * CHUNK
+            for h in range(CHUNK // BANK_PIXELS):
+                result = store_pool.tile([P, BANK_TILES, OUT_CH], F32, name="result")
+                nc.vector.tensor_tensor(out=result[:], in0=acc_of[chunk][h][:], in1=bias[:], op=ALU.add)
                 stored = first_pixel + h * BANK_PIXELS
                 nc.sync.dma_start(
                     out=out[b, stored : stored + BANK_PIXELS, :].rearrange("(g p) o -> p g o", p=PIXEL_TILE),
                     in_=result[:],
                 )
 
-        prepare(0)
-        for b in range(BATCH):
-            if b + 1 < BATCH:
-                prepare(b + 1)
-            for j in range(CHUNKS):
-                convolve(b, j)
+        for tick in range(-LEAD, ALL_CHUNKS):
+            step = tick + LEAD
+            row, half = step // 2, step % 2
+            if step == NORM_STEP - 2:
+                nc.vector.quantize_mx(
+                    out=w_codes[:].bitcast(FP8X4),
+                    scales=w_scales[:],
+                    in_=w_grouped[:].rearrange("q o t -> q (o t)"),
+                )
+            if tick == -1:
+                for g in range(BANK_TILES):
+                    nc.vector.tensor_copy(out=bias[:, g, :], in_=bias_bf16[:])
+            since = step - NORM_STEP
+            if since >= 0 and since // (2 * PACK) < BATCH and since % (2 * PACK) in (0, 2):
+                b = since // (2 * PACK)
+                if since % (2 * PACK) == 0:
+                    nc.vector.reciprocal(out=rstd[:, b * PACK : (b + 1) * PACK], in_=std[:, b * PACK : (b + 1) * PACK])
+                normalise(b, since % (2 * PACK) // 2)
+            if 0 <= tick + 1 < ALL_CHUNKS:
+                quantise_and_multiply(tick + 1)
+            if 0 <= tick + 1 + RING < ALL_CHUNKS:
+                if row >= ROWS:
+                    pool_pixels = POOL_LAST
+                elif vector_alone(row) or (half == 0 and kind_of(row) == "shared"):
+                    pool_pixels = POOL_LONG
+                else:
+                    pool_pixels = POOL_SHORT
+                regroup(tick + 1 + RING, pool_pixels)
+            if 0 <= tick:
+                add_bias_and_store(tick)
+            if half == 0 and row + 1 < ROWS and kind_of(row + 1) == "tensor":
+                tensor_fold(row + 1)
+            if row < ROWS:
+                vector_statistics(row, half)
+                if half == 0 and kind_of(row) in ("scalar", "tensor"):
+                    scalar_mean(row)
+                if half == 1 and not vector_alone(row):
+                    scalar_squares(row)
+            if half == 0 and 1 <= row <= ROWS:
+                scalar_std(row - 1)

@@ -31,11 +31,11 @@ RUN = 4
 PIXEL_TILE = P
 BANK_TILES = 2
 BANK_PIXELS = BANK_TILES * PIXEL_TILE
-RING = 3
-POOL_LONG = 448
-POOL_SHORT = 256
-POOL_LAST = 128
-NORM_STEP = 12
+RING = 4
+POOL_LONG = 384
+POOL_SHORT = 160
+POOL_LAST = 160
+NORM_STEP = 13
 FOLD = 512
 LEAD = NORM_STEP + 1 + RING
 
@@ -106,6 +106,7 @@ def tile_adaattn_pa_t_kernel(tc, c_1x, f_w, f_b, out):
             if b == 1:
                 nc.sync.dma_start(out=bias_bf16[:], in_=f_b.partition_broadcast(P))
 
+        half_mean = const.tile([P, ROWS], F32)
         mean = const.tile([P, ROWS], F32)
         squares = const.tile([P, ROWS], F32)
         mean_var = const.tile([P, ROWS, 2], F32)
@@ -133,16 +134,16 @@ def tile_adaattn_pa_t_kernel(tc, c_1x, f_w, f_b, out):
                     nc.vector.bn_stats(out=stats[:, s, :], in_=x_row(row)[:, s * STAT_SLICE : (s + 1) * STAT_SLICE])
                 if half == 1:
                     nc.vector.bn_aggr(out=mean_var[:, row, :], in_=stats[:].rearrange("p s k -> p (s k)"))
-            elif half == 0 and kind_of(row) == "shared":
-                unread = scratch.tile([P, PIXELS], BF16, name="unread_v")
+            elif kind_of(row) == "shared":
+                unread = scratch.tile([P, PIXELS // 2], BF16, name="unread_v")
                 nc.vector.tensor_scalar(
                     out=unread[:],
-                    in0=x_row(row),
+                    in0=x_row(row)[:, half * (PIXELS // 2) : (half + 1) * (PIXELS // 2)],
                     scalar1=1.0 / PIXELS,
-                    scalar2=None,
+                    scalar2=None if half == 0 else half_mean[:, row : row + 1],
                     op0=ALU.mult,
                     op1=ALU.add,
-                    accum_out=mean[:, row : row + 1],
+                    accum_out=half_mean[:, row : row + 1] if half == 0 else mean[:, row : row + 1],
                 )
 
         def tensor_fold(row):
@@ -204,10 +205,11 @@ def tile_adaattn_pa_t_kernel(tc, c_1x, f_w, f_b, out):
             grouped = group_pool.tile([P, CHUNK, PACK], BF16, align_bytes=64, name="grouped")
             grouped_of[chunk] = grouped
             split = CHUNK - pool_pixels
-            nc.scalar.copy(
-                out=grouped[:, :split, :].rearrange("p (c i) t -> p c t i", i=RUN),
-                in_=x_tiles[b][:, :, first_pixel : first_pixel + split].rearrange("p t (c i) -> p c t i", i=RUN),
-            )
+            if split > 0:
+                nc.scalar.copy(
+                    out=grouped[:, :split, :].rearrange("p (c i) t -> p c t i", i=RUN),
+                    in_=x_tiles[b][:, :, first_pixel : first_pixel + split].rearrange("p t (c i) -> p c t i", i=RUN),
+                )
             nc.gpsimd.tensor_scalar(
                 out=grouped[:, split:, :],
                 in0=x_tiles[b][:, :, first_pixel + split : first_pixel + CHUNK].rearrange("p t w -> p w t"),
@@ -275,11 +277,15 @@ def tile_adaattn_pa_t_kernel(tc, c_1x, f_w, f_b, out):
             if 0 <= tick + 1 + RING < ALL_CHUNKS:
                 if row >= ROWS:
                     pool_pixels = POOL_LAST
-                elif vector_alone(row) or (half == 0 and kind_of(row) == "shared"):
+                elif kind_of(row) in ("vector", "shared"):
                     pool_pixels = POOL_LONG
                 else:
                     pool_pixels = POOL_SHORT
                 regroup(tick + 1 + RING, pool_pixels)
+            if half == 0 and 1 <= row <= ROWS and kind_of(row - 1) == "shared":
+                scalar_squares(row - 1)
+            if half == 1 and 1 <= row <= ROWS:
+                scalar_std(row - 1)
             if 0 <= tick:
                 add_bias_and_store(tick)
             if half == 0 and row + 1 < ROWS and kind_of(row + 1) == "tensor":
@@ -288,7 +294,5 @@ def tile_adaattn_pa_t_kernel(tc, c_1x, f_w, f_b, out):
                 vector_statistics(row, half)
                 if half == 0 and kind_of(row) in ("scalar", "tensor"):
                     scalar_mean(row)
-                if half == 1 and not vector_alone(row):
+                if half == 1 and kind_of(row) in ("scalar", "tensor"):
                     scalar_squares(row)
-            if half == 0 and 1 <= row <= ROWS:
-                scalar_std(row - 1)

@@ -27,7 +27,7 @@ CHUNKS = PIXELS // CHUNK
 ALL_CHUNKS = BATCH * CHUNKS
 NORM_PIECES = 2
 NORM_PIXELS = PIXELS // NORM_PIECES
-RUN = 4
+RUN = 8
 PIXEL_TILE = P
 BANK_TILES = 2
 BANK_PIXELS = BANK_TILES * PIXEL_TILE

@@ -211,8 +211,8 @@ def tile_adaattn_pa_t_kernel(tc, c_1x, f_w, f_b, out):
                     in_=x_tiles[b][:, :, first_pixel : first_pixel + split].rearrange("p t (c i) -> p c t i", i=RUN),
                 )
             nc.gpsimd.tensor_scalar(
-                out=grouped[:, split:, :],
-                in0=x_tiles[b][:, :, first_pixel + split : first_pixel + CHUNK].rearrange("p t w -> p w t"),
+                out=grouped[:, split:, :].rearrange("p (c i) t -> p c t i", i=RUN),
+                in0=x_tiles[b][:, :, first_pixel + split : first_pixel + CHUNK].rearrange("p t (c i) -> p c t i", i=RUN),
                 scalar1=1.0,
                 scalar2=0.0,
                 op0=ALU.mult,

@@ -20,6 +20,7 @@ OUT_CH = 256
 EPS = 1e-5
 
 LOAD_PIECES = 2
+FIRST_PIECES = 8
 STAT_SLICE = 512
 STAT_SLICES = PIXELS // STAT_SLICE
 CHUNK = 512
@@ -54,9 +55,10 @@ def vector_alone(row):
 
 def load_batch(nc, x_tile, c_1x, b):
     rows = c_1x[b, :, :, :].rearrange("(p t) h w -> t p (h w)", t=PACK)
-    piece = PIXELS // LOAD_PIECES
     for t in range(PACK):
-        for i in range(LOAD_PIECES):
+        pieces = FIRST_PIECES if b == 0 and t == 0 else LOAD_PIECES
+        piece = PIXELS // pieces
+        for i in range(pieces):
             pixels = slice(i * piece, (i + 1) * piece)
             nc.sync.dma_start(out=x_tile[:, t, pixels], in_=rows[t, :, pixels])
 

@@ -26,8 +26,6 @@ STAT_SLICES = PIXELS // STAT_SLICE
 CHUNK = 512
 CHUNKS = PIXELS // CHUNK
 ALL_CHUNKS = BATCH * CHUNKS
-NORM_PIECES = 2
-NORM_PIXELS = PIXELS // NORM_PIECES
 RUN = 8
 PIXEL_TILE = P
 BANK_TILES = 2
@@ -189,13 +187,12 @@ def tile_adaattn_pa_t_kernel(tc, c_1x, f_w, f_b, out):
                 spread, factor = squares[:, row : row + 1], 1.0 / (PIXELS - 1.0)
             nc.scalar.activation(out=std[:, row : row + 1], in_=spread, func=ACT.Sqrt, scale=factor, bias=EPS)
 
-        def normalise(b, piece):
-            pixels = slice(piece * NORM_PIXELS, (piece + 1) * NORM_PIXELS)
+        def normalise(b):
             for t in range(PACK):
                 row = b * PACK + t
                 nc.vector.tensor_scalar(
-                    out=x_tiles[b][:, t, pixels],
-                    in0=x_tiles[b][:, t, pixels],
+                    out=x_tiles[b][:, t, :],
+                    in0=x_tiles[b][:, t, :],
                     scalar1=mean_of(row),
                     scalar2=rstd[:, row : row + 1],
                     op0=ALU.subtract,
@@ -269,11 +266,10 @@ def tile_adaattn_pa_t_kernel(tc, c_1x, f_w, f_b, out):
                 for g in range(BANK_TILES):
                     nc.vector.tensor_copy(out=bias[:, g, :], in_=bias_bf16[:])
             since = step - NORM_STEP
-            if since >= 0 and since // (2 * PACK) < BATCH and since % (2 * PACK) in (0, 2):
+            if since >= 0 and since // (2 * PACK) < BATCH and since % (2 * PACK) == 0:
                 b = since // (2 * PACK)
-                if since % (2 * PACK) == 0:
-                    nc.vector.reciprocal(out=rstd[:, b * PACK : (b + 1) * PACK], in_=std[:, b * PACK : (b + 1) * PACK])
-                normalise(b, since % (2 * PACK) // 2)
+                nc.vector.reciprocal(out=rstd[:, b * PACK : (b + 1) * PACK], in_=std[:, b * PACK : (b + 1) * PACK])
+                normalise(b)
             if 0 <= tick + 1 < ALL_CHUNKS:
                 quantise_and_multiply(tick + 1)
             if 0 <= tick + 1 + RING < ALL_CHUNKS:

@@ -32,7 +32,7 @@ BANK_TILES = 2
 BANK_PIXELS = BANK_TILES * PIXEL_TILE
 RING = 4
 POOL_LONG = 384
-POOL_SHORT = 160
+POOL_SHORT = 192
 POOL_LAST = 160
 NORM_STEP = 13
 FOLD = 512

@@ -210,8 +210,8 @@ def tile_adaattn_pa_t_kernel(tc, c_1x, f_w, f_b, out):
                     in_=x_tiles[b][:, :, first_pixel : first_pixel + split].rearrange("p t (c i) -> p c t i", i=RUN),
                 )
             nc.gpsimd.tensor_scalar(
-                out=grouped[:, split:, :].rearrange("p (c i) t -> p c t i", i=RUN),
-                in0=x_tiles[b][:, :, first_pixel + split : first_pixel + CHUNK].rearrange("p t (c i) -> p c t i", i=RUN),
+                out=grouped[:, split:, :],
+                in0=x_tiles[b][:, :, first_pixel + split : first_pixel + CHUNK].rearrange("p t c -> p c t"),
                 scalar1=1.0,
                 scalar2=0.0,
                 op0=ALU.mult,

@@ -38,12 +38,17 @@ NORM_STEP = 13
 FOLD = 512
 LEAD = NORM_STEP + 1 + RING
 
+POOL_ROW = PACK + 1
+W_STEP = 2
+
 FLOPS = 2 * BATCH * PIXELS * P * PACK * OUT_CH
 
 
 def kind_of(row):
     if row < PACK:
         return "scalar" if row == 1 else "vector"
+    if row == POOL_ROW:
+        return "pool"
     return "tensor" if row % PACK == 0 else "shared"
 
 
@@ -51,14 +56,14 @@ def vector_alone(row):
     return kind_of(row) == "vector"
 
 
-def load_batch(nc, x_tile, c_1x, b):
+def load_row(nc, x_tiles, c_1x, row):
+    b, t = row // PACK, row % PACK
     rows = c_1x[b, :, :, :].rearrange("(p t) h w -> t p (h w)", t=PACK)
-    for t in range(PACK):
-        pieces = FIRST_PIECES if b == 0 and t == 0 else LOAD_PIECES
-        piece = PIXELS // pieces
-        for i in range(pieces):
-            pixels = slice(i * piece, (i + 1) * piece)
-            nc.sync.dma_start(out=x_tile[:, t, pixels], in_=rows[t, :, pixels])
+    pieces = FIRST_PIECES if row == 0 else LOAD_PIECES
+    piece = PIXELS // pieces
+    for i in range(pieces):
+        pixels = slice(i * piece, (i + 1) * piece)
+        nc.sync.dma_start(out=x_tiles[b][:, t, pixels], in_=rows[t, :, pixels])
 
 
 def turn_weights(nc, const, psum_w, f_w):
@@ -93,6 +98,10 @@ def tile_adaattn_pa_t_kernel(tc, c_1x, f_w, f_b, out):
         psum = ctx.enter_context(tc.psum_pool(name="psum", bufs=6))
         ctx.enter_context(tc.manual_schedule())
 
+        one = const.tile([P, 1], F32)
+        nc.vector.memset(one[:], 1.0)
+        unread_root = const.tile([P, 1], F32)
+        nc.scalar.activation(out=unread_root[:], in_=one[:], func=ACT.Sqrt)
         w_grouped, identity = turn_weights(nc, const, psum_w, f_w)
         w_codes = const.tile([P, OUT_CH], U32, align_bytes=64)
         w_scales = const.tile([P, OUT_CH], U8, align_bytes=64)
@@ -101,15 +110,17 @@ def tile_adaattn_pa_t_kernel(tc, c_1x, f_w, f_b, out):
         x_tiles = []
         for b in range(BATCH):
             x_tile = x_pool.tile([P, PACK, PIXELS], BF16)
-            load_batch(nc, x_tile, c_1x, b)
             x_tiles.append(x_tile)
-            if b == 1:
+        for row in list(range(PACK - 1)) + [POOL_ROW] + [row for row in range(PACK - 1, ROWS) if row != POOL_ROW]:
+            load_row(nc, x_tiles, c_1x, row)
+            if row == 2 * PACK - 1:
                 nc.sync.dma_start(out=bias_bf16[:], in_=f_b.partition_broadcast(P))
 
         half_mean = const.tile([P, ROWS], F32)
         mean = const.tile([P, ROWS], F32)
         squares = const.tile([P, ROWS], F32)
         mean_var = const.tile([P, ROWS, 2], F32)
+        pool_folded = const.tile([P, FOLD], F32)
         std = const.tile([P, ROWS], F32)
         rstd = const.tile([P, ROWS], F32)
         grouped_of = {}
@@ -146,6 +157,20 @@ def tile_adaattn_pa_t_kernel(tc, c_1x, f_w, f_b, out):
                     accum_out=half_mean[:, row : row + 1] if half == 0 else mean[:, row : row + 1],
                 )
 
+        def pool_fold(row):
+            quarter = PIXELS // 4
+            halves = const.tile([P, 2, quarter], F32)
+            for i in range(2):
+                nc.gpsimd.tensor_tensor(
+                    out=halves[:, i, :],
+                    in0=x_row(row)[:, 2 * i * quarter : (2 * i + 1) * quarter],
+                    in1=x_row(row)[:, (2 * i + 1) * quarter : (2 * i + 2) * quarter],
+                    op=ALU.add,
+                )
+            whole = const.tile([P, quarter], F32)
+            nc.gpsimd.tensor_tensor(out=whole[:], in0=halves[:, 0, :], in1=halves[:, 1, :], op=ALU.add)
+            nc.gpsimd.tensor_tensor(out=pool_folded[:], in0=whole[:, :FOLD], in1=whole[:, FOLD:], op=ALU.add)
+
         def tensor_fold(row):
             folded = psum_f.tile([P, FOLD], F32, name="folded")
             grouped_of["folded"] = folded
@@ -159,7 +184,8 @@ def tile_adaattn_pa_t_kernel(tc, c_1x, f_w, f_b, out):
                 )
 
         def scalar_mean(row):
-            source = grouped_of["folded"][:] if kind_of(row) == "tensor" else x_row(row)
+            source = {"tensor": grouped_of.get("folded"), "pool": pool_folded}.get(kind_of(row))
+            source = x_row(row) if source is None else source[:]
             unread = scratch.tile([P, PIXELS], BF16, name="unread_s")
             nc.scalar.activation(
                 out=unread[:, : source.shape[1]],
@@ -182,10 +208,15 @@ def tile_adaattn_pa_t_kernel(tc, c_1x, f_w, f_b, out):
 
         def scalar_std(row):
             if vector_alone(row):
-                spread, factor = mean_var[:, row, 1:2], PIXELS / (PIXELS - 1.0)
+                spread, factor, rows = mean_var[:, row, 1:2], PIXELS / (PIXELS - 1.0), slice(row, row + 1)
+            elif row < PACK:
+                spread, factor, rows = squares[:, row : row + 1], 1.0 / (PIXELS - 1.0), slice(row, row + 1)
+            elif row % PACK == PACK - 1:
+                rows = slice(row + 1 - PACK, row + 1)
+                spread, factor = squares[:, rows], 1.0 / (PIXELS - 1.0)
             else:
-                spread, factor = squares[:, row : row + 1], 1.0 / (PIXELS - 1.0)
-            nc.scalar.activation(out=std[:, row : row + 1], in_=spread, func=ACT.Sqrt, scale=factor, bias=EPS)
+                return
+            nc.scalar.activation(out=std[:, rows], in_=spread, func=ACT.Sqrt, scale=factor, bias=EPS)
 
         def normalise(b):
             for t in range(PACK):
@@ -210,8 +241,8 @@ def tile_adaattn_pa_t_kernel(tc, c_1x, f_w, f_b, out):
                     in_=x_tiles[b][:, :, first_pixel : first_pixel + split].rearrange("p t (c i) -> p c t i", i=RUN),
                 )
             nc.gpsimd.tensor_scalar(
-                out=grouped[:, split:, :],
-                in0=x_tiles[b][:, :, first_pixel + split : first_pixel + CHUNK].rearrange("p t c -> p c t"),
+                out=grouped[:, split:, :].rearrange("p (c i) t -> p c t i", i=RUN),
+                in0=x_tiles[b][:, :, first_pixel + split : first_pixel + CHUNK].rearrange("p t (c i) -> p c t i", i=RUN),
                 scalar1=1.0,
                 scalar2=0.0,
                 op0=ALU.mult,
@@ -253,10 +284,11 @@ def tile_adaattn_pa_t_kernel(tc, c_1x, f_w, f_b, out):
                     in_=result[:],
                 )
 
+        pool_fold(POOL_ROW)
         for tick in range(-LEAD, ALL_CHUNKS):
             step = tick + LEAD
             row, half = step // 2, step % 2
-            if step == NORM_STEP - 2:
+            if step == W_STEP:
                 nc.vector.quantize_mx(
                     out=w_codes[:].bitcast(FP8X4),
                     scales=w_scales[:],
@@ -282,7 +314,8 @@ def tile_adaattn_pa_t_kernel(tc, c_1x, f_w, f_b, out):
                 regroup(tick + 1 + RING, pool_pixels)
             if half == 0 and 1 <= row <= ROWS and kind_of(row - 1) == "shared":
                 scalar_squares(row - 1)
-            if half == 1 and 1 <= row <= ROWS:
+                scalar_std(row - 1)
+            if half == 1 and 1 <= row <= ROWS and kind_of(row - 1) == "vector":
                 scalar_std(row - 1)
             if 0 <= tick:
                 add_bias_and_store(tick)
@@ -290,7 +323,8 @@ def tile_adaattn_pa_t_kernel(tc, c_1x, f_w, f_b, out):
                 tensor_fold(row + 1)
             if row < ROWS:
                 vector_statistics(row, half)
-                if half == 0 and kind_of(row) in ("scalar", "tensor"):
+                if half == 0 and kind_of(row) in ("scalar", "tensor", "pool"):
                     scalar_mean(row)
-                if half == 1 and kind_of(row) in ("scalar", "tensor"):
+                if half == 1 and kind_of(row) in ("scalar", "tensor", "pool"):
                     scalar_squares(row)
+                    scalar_std(row)

from contextlib import ExitStack

import concourse.mybir as mybir
from concourse.masks import make_identity

BF16 = mybir.dt.bfloat16
F32 = mybir.dt.float32
U32 = mybir.dt.uint32
U8 = mybir.dt.uint8
FP8X4 = mybir.dt.float8_e4m3fn_x4
ALU = mybir.AluOpType
ACT = mybir.ActivationFunctionType

P = 128
PACK = 4
BATCH = 4
ROWS = BATCH * PACK
PIXELS = 64 * 64
OUT_CH = 256
EPS = 1e-5

LOAD_PIECES = 2
FIRST_PIECES = 8
STAT_SLICE = 512
STAT_SLICES = PIXELS // STAT_SLICE
CHUNK = 512
CHUNKS = PIXELS // CHUNK
ALL_CHUNKS = BATCH * CHUNKS
RUN = 8
PIXEL_TILE = P
BANK_TILES = 2
BANK_PIXELS = BANK_TILES * PIXEL_TILE
RING = 4
POOL_LONG = 384
POOL_SHORT = 192
POOL_LAST = 160
NORM_STEP = 13
FOLD = 512
LEAD = NORM_STEP + 1 + RING

POOL_ROW = PACK + 1
W_STEP = 2

FLOPS = 2 * BATCH * PIXELS * P * PACK * OUT_CH


def kind_of(row):
    if row < PACK:
        return "scalar" if row == 1 else "vector"
    if row == POOL_ROW:
        return "pool"
    return "tensor" if row % PACK == 0 else "shared"


def vector_alone(row):
    return kind_of(row) == "vector"


def load_row(nc, x_tiles, c_1x, row):
    b, t = row // PACK, row % PACK
    rows = c_1x[b, :, :, :].rearrange("(p t) h w -> t p (h w)", t=PACK)
    pieces = FIRST_PIECES if row == 0 else LOAD_PIECES
    piece = PIXELS // pieces
    for i in range(pieces):
        pixels = slice(i * piece, (i + 1) * piece)
        nc.sync.dma_start(out=x_tiles[b][:, t, pixels], in_=rows[t, :, pixels])


def turn_weights(nc, const, psum_w, f_w):
    halves = OUT_CH // P
    w_rows = const.tile([P, halves, P * PACK], BF16)
    nc.scalar.dma_start(out=w_rows[:], in_=f_w.rearrange("(h o) c -> o h c", h=halves))
    identity = const.tile([P, P], BF16)
    make_identity(nc, identity[:])
    w_sorted = const.tile([P, halves, PACK, P], BF16)
    nc.scalar.copy(out=w_sorted[:], in_=w_rows[:].rearrange("o h (q t) -> o h t q", t=PACK))
    w_turned = psum_w.tile([P, PACK, OUT_CH], BF16)
    for h in range(halves):
        for t in range(PACK):
            nc.tensor.transpose(w_turned[:, t, h * P : (h + 1) * P], w_sorted[:, h, t, :], identity[:])
    w_grouped = const.tile([P, OUT_CH, PACK], BF16, align_bytes=64)
    nc.scalar.copy(out=w_grouped[:], in_=w_turned[:].rearrange("q t o -> q o t"))
    return w_grouped, identity


def tile_adaattn_pa_t_kernel(tc, c_1x, f_w, f_b, out):
    nc = tc.nc
    with ExitStack() as ctx:
        const = ctx.enter_context(tc.tile_pool(name="const", bufs=1))
        x_pool = ctx.enter_context(tc.tile_pool(name="x", bufs=BATCH))
        small = ctx.enter_context(tc.tile_pool(name="small", bufs=2))
        scratch = ctx.enter_context(tc.tile_pool(name="scratch", bufs=2))
        group_pool = ctx.enter_context(tc.tile_pool(name="grouped", bufs=RING))
        stage = ctx.enter_context(tc.tile_pool(name="stage", bufs=3))
        store_pool = ctx.enter_context(tc.tile_pool(name="stored", bufs=6))
        psum_w = ctx.enter_context(tc.psum_pool(name="psum_w", bufs=1))
        psum_f = ctx.enter_context(tc.psum_pool(name="psum_f", bufs=1))
        psum = ctx.enter_context(tc.psum_pool(name="psum", bufs=6))
        ctx.enter_context(tc.manual_schedule())

        one = const.tile([P, 1], F32)
        nc.vector.memset(one[:], 1.0)
        unread_root = const.tile([P, 1], F32)
        nc.scalar.activation(out=unread_root[:], in_=one[:], func=ACT.Sqrt)
        w_grouped, identity = turn_weights(nc, const, psum_w, f_w)
        w_codes = const.tile([P, OUT_CH], U32, align_bytes=64)
        w_scales = const.tile([P, OUT_CH], U8, align_bytes=64)
        bias_bf16 = const.tile([P, OUT_CH], BF16)
        bias = const.tile([P, BANK_TILES, OUT_CH], F32)
        x_tiles = []
        for b in range(BATCH):
            x_tile = x_pool.tile([P, PACK, PIXELS], BF16)
            x_tiles.append(x_tile)
        for row in list(range(PACK - 1)) + [POOL_ROW] + [row for row in range(PACK - 1, ROWS) if row != POOL_ROW]:
            load_row(nc, x_tiles, c_1x, row)
            if row == 2 * PACK - 1:
                nc.sync.dma_start(out=bias_bf16[:], in_=f_b.partition_broadcast(P))

        half_mean = const.tile([P, ROWS], F32)
        mean = const.tile([P, ROWS], F32)
        squares = const.tile([P, ROWS], F32)
        mean_var = const.tile([P, ROWS, 2], F32)
        pool_folded = const.tile([P, FOLD], F32)
        std = const.tile([P, ROWS], F32)
        rstd = const.tile([P, ROWS], F32)
        grouped_of = {}
        codes_of = {}
        acc_of = {}

        def x_row(row):
            return x_tiles[row // PACK][:, row % PACK, :]

        def mean_of(row):
            if vector_alone(row):
                return mean_var[:, row, 0:1]
            return mean[:, row : row + 1]

        def vector_statistics(row, half):
            if vector_alone(row):
                if half == 0:
                    stats = small.tile([P, STAT_SLICES, 6], F32, name="stats")
                    grouped_of["stats"] = stats
                stats = grouped_of["stats"]
                for s in range(half * STAT_SLICES // 2, (half + 1) * STAT_SLICES // 2):
                    nc.vector.bn_stats(out=stats[:, s, :], in_=x_row(row)[:, s * STAT_SLICE : (s + 1) * STAT_SLICE])
                if half == 1:
                    nc.vector.bn_aggr(out=mean_var[:, row, :], in_=stats[:].rearrange("p s k -> p (s k)"))
            elif kind_of(row) == "shared":
                unread = scratch.tile([P, PIXELS // 2], BF16, name="unread_v")
                nc.vector.tensor_scalar(
                    out=unread[:],
                    in0=x_row(row)[:, half * (PIXELS // 2) : (half + 1) * (PIXELS // 2)],
                    scalar1=1.0 / PIXELS,
                    scalar2=None if half == 0 else half_mean[:, row : row + 1],
                    op0=ALU.mult,
                    op1=ALU.add,
                    accum_out=half_mean[:, row : row + 1] if half == 0 else mean[:, row : row + 1],
                )

        def pool_fold(row):
            quarter = PIXELS // 4
            halves = const.tile([P, 2, quarter], F32)
            for i in range(2):
                nc.gpsimd.tensor_tensor(
                    out=halves[:, i, :],
                    in0=x_row(row)[:, 2 * i * quarter : (2 * i + 1) * quarter],
                    in1=x_row(row)[:, (2 * i + 1) * quarter : (2 * i + 2) * quarter],
                    op=ALU.add,
                )
            whole = const.tile([P, quarter], F32)
            nc.gpsimd.tensor_tensor(out=whole[:], in0=halves[:, 0, :], in1=halves[:, 1, :], op=ALU.add)
            nc.gpsimd.tensor_tensor(out=pool_folded[:], in0=whole[:, :FOLD], in1=whole[:, FOLD:], op=ALU.add)

        def tensor_fold(row):
            folded = psum_f.tile([P, FOLD], F32, name="folded")
            grouped_of["folded"] = folded
            for s in range(PIXELS // FOLD):
                nc.tensor.matmul(
                    out=folded[:],
                    lhsT=identity[:],
                    rhs=x_row(row)[:, s * FOLD : (s + 1) * FOLD],
                    start=(s == 0),
                    stop=(s == PIXELS // FOLD - 1),
                )

        def scalar_mean(row):
            source = {"tensor": grouped_of.get("folded"), "pool": pool_folded}.get(kind_of(row))
            source = x_row(row) if source is None else source[:]
            unread = scratch.tile([P, PIXELS], BF16, name="unread_s")
            nc.scalar.activation(
                out=unread[:, : source.shape[1]],
                in_=source,
                func=ACT.Identity,
                scale=1.0 / PIXELS,
                accum_out=mean[:, row : row + 1],
            )

        def scalar_squares(row):
            unread = scratch.tile([P, PIXELS], BF16, name="unread_s")
            nc.scalar.activation(
                out=unread[:],
                in_=x_row(row),
                func=ACT.Square,
                scale=-1.0,
                bias=mean[:, row : row + 1],
                accum_out=squares[:, row : row + 1],
            )

        def scalar_std(row):
            if vector_alone(row):
                spread, factor, rows = mean_var[:, row, 1:2], PIXELS / (PIXELS - 1.0), slice(row, row + 1)
            elif row < PACK:
                spread, factor, rows = squares[:, row : row + 1], 1.0 / (PIXELS - 1.0), slice(row, row + 1)
            elif row % PACK == PACK - 1:
                rows = slice(row + 1 - PACK, row + 1)
                spread, factor = squares[:, rows], 1.0 / (PIXELS - 1.0)
            else:
                return
            nc.scalar.activation(out=std[:, rows], in_=spread, func=ACT.Sqrt, scale=factor, bias=EPS)

        def normalise(b):
            for t in range(PACK):
                row = b * PACK + t
                nc.vector.tensor_scalar(
                    out=x_tiles[b][:, t, :],
                    in0=x_tiles[b][:, t, :],
                    scalar1=mean_of(row),
                    scalar2=rstd[:, row : row + 1],
                    op0=ALU.subtract,
                    op1=ALU.mult,
                )

        def regroup(chunk, pool_pixels):
            b, first_pixel = chunk // CHUNKS, (chunk % CHUNKS) * CHUNK
            grouped = group_pool.tile([P, CHUNK, PACK], BF16, align_bytes=64, name="grouped")
            grouped_of[chunk] = grouped
            split = CHUNK - pool_pixels
            if split > 0:
                nc.scalar.copy(
                    out=grouped[:, :split, :].rearrange("p (c i) t -> p c t i", i=RUN),
                    in_=x_tiles[b][:, :, first_pixel : first_pixel + split].rearrange("p t (c i) -> p c t i", i=RUN),
                )
            nc.gpsimd.tensor_scalar(
                out=grouped[:, split:, :].rearrange("p (c i) t -> p c t i", i=RUN),
                in0=x_tiles[b][:, :, first_pixel + split : first_pixel + CHUNK].rearrange("p t (c i) -> p c t i", i=RUN),
                scalar1=1.0,
                scalar2=0.0,
                op0=ALU.mult,
                op1=ALU.add,
            )

        def quantise_and_multiply(chunk):
            codes = stage.tile([P, CHUNK], U32, align_bytes=64, name="codes")
            scales = stage.tile([P, CHUNK], U8, align_bytes=64, name="scales")
            nc.vector.quantize_mx(
                out=codes[:].bitcast(FP8X4),
                scales=scales[:],
                in_=grouped_of[chunk][:].rearrange("p w t -> p (w t)"),
            )
            acc_of[chunk] = []
            for h in range(CHUNK // BANK_PIXELS):
                acc = psum.tile([P, BANK_TILES, OUT_CH], F32, name="acc")
                acc_of[chunk].append(acc)
                for g in range(BANK_TILES):
                    first = h * BANK_PIXELS + g * PIXEL_TILE
                    nc.tensor.matmul_mx(
                        out=acc[:, g, :],
                        lhsT=codes[:, first : first + PIXEL_TILE].bitcast(FP8X4),
                        lhsT_scale=scales[:, first : first + PIXEL_TILE],
                        rhs=w_codes[:].bitcast(FP8X4),
                        rhs_scale=w_scales[:],
                        start=True,
                        stop=True,
                    )

        def add_bias_and_store(chunk):
            b, first_pixel = chunk // CHUNKS, (chunk % CHUNKS) * CHUNK
            for h in range(CHUNK // BANK_PIXELS):
                result = store_pool.tile([P, BANK_TILES, OUT_CH], F32, name="result")
                nc.vector.tensor_tensor(out=result[:], in0=acc_of[chunk][h][:], in1=bias[:], op=ALU.add)
                stored = first_pixel + h * BANK_PIXELS
                nc.sync.dma_start(
                    out=out[b, stored : stored + BANK_PIXELS, :].rearrange("(g p) o -> p g o", p=PIXEL_TILE),
                    in_=result[:],
                )

        pool_fold(POOL_ROW)
        for tick in range(-LEAD, ALL_CHUNKS):
            step = tick + LEAD
            row, half = step // 2, step % 2
            if step == W_STEP:
                nc.vector.quantize_mx(
                    out=w_codes[:].bitcast(FP8X4),
                    scales=w_scales[:],
                    in_=w_grouped[:].rearrange("q o t -> q (o t)"),
                )
            if tick == -1:
                for g in range(BANK_TILES):
                    nc.vector.tensor_copy(out=bias[:, g, :], in_=bias_bf16[:])
            since = step - NORM_STEP
            if since >= 0 and since // (2 * PACK) < BATCH and since % (2 * PACK) == 0:
                b = since // (2 * PACK)
                nc.vector.reciprocal(out=rstd[:, b * PACK : (b + 1) * PACK], in_=std[:, b * PACK : (b + 1) * PACK])
                normalise(b)
            if 0 <= tick + 1 < ALL_CHUNKS:
                quantise_and_multiply(tick + 1)
            if 0 <= tick + 1 + RING < ALL_CHUNKS:
                if row >= ROWS:
                    pool_pixels = POOL_LAST
                elif kind_of(row) in ("vector", "shared"):
                    pool_pixels = POOL_LONG
                else:
                    pool_pixels = POOL_SHORT
                regroup(tick + 1 + RING, pool_pixels)
            if half == 0 and 1 <= row <= ROWS and kind_of(row - 1) == "shared":
                scalar_squares(row - 1)
                scalar_std(row - 1)
            if half == 1 and 1 <= row <= ROWS and kind_of(row - 1) == "vector":
                scalar_std(row - 1)
            if 0 <= tick:
                add_bias_and_store(tick)
            if half == 0 and row + 1 < ROWS and kind_of(row + 1) == "tensor":
                tensor_fold(row + 1)
            if row < ROWS:
                vector_statistics(row, half)
                if half == 0 and kind_of(row) in ("scalar", "tensor", "pool"):
                    scalar_mean(row)
                if half == 1 and kind_of(row) in ("scalar", "tensor", "pool"):
                    scalar_squares(row)
                    scalar_std(row)
